import numpy as np
import ml_dtypes


def mxq(x, axis, fmt="e4m3"):
    dtype, down = {"e4m3": (ml_dtypes.float8_e4m3fn, 7), "e5m2": (ml_dtypes.float8_e5m2, 14)}[fmt]
    v = np.moveaxis(np.asarray(x, np.float32).astype(ml_dtypes.bfloat16).astype(np.float64), axis, -1)
    blocks = v.reshape(v.shape[:-1] + (-1, 32))
    amax = np.abs(blocks).max(-1, keepdims=True)
    byte = np.maximum(np.where(amax > 0, np.frexp(amax)[1] - 1 + 127, 0) - down, 1)
    scale = np.exp2(byte - 127.0)
    codes = (blocks / scale).astype(np.float32).astype(dtype).astype(np.float64)
    return np.moveaxis((codes * scale).reshape(v.shape), -1, axis)


WIDE = False


def mx_kscale(k):
    if not WIDE:
        return np.ones(k)
    levels = np.array([10, -10, 5, -5, 0])
    if k % 512:
        return np.exp2(np.random.permutation(np.resize(levels, k // 32))).repeat(32)
    a = np.empty((k // 512, 16))
    for p in range(k // 512):
        a[p, :8] = np.random.permutation(np.resize(levels, 8))
        for g in range(8):
            far = levels[np.abs(levels - a[p, g]) >= 10]
            a[p, g + 8] = far[np.random.randint(len(far))]
    return np.exp2(a.ravel()).repeat(32)


BF16 = ml_dtypes.bfloat16


def bf(x):
    return np.asarray(x, np.float32).astype(BF16)


def f64(x):
    return np.asarray(x).astype(np.float64)


B, T, D, E, H, L = 128, 10, 1024, 128, 128, 2
TM = T - L
F = H + L * D + 1


def setup_inputs():
    s = mx_kscale(D)
    we = np.random.standard_normal((D, H)) / np.sqrt(H)
    wy = np.random.standard_normal((D, L, D)) * 0.7 / np.sqrt(L * D) / s
    wx = np.random.standard_normal((D, 1)) * 0.5 / s[:, None]
    return {"x": bf(np.random.standard_normal((B, T, D)) * s),
            "emb": bf(np.random.standard_normal((B, H)) * 0.5),
            "Wg": bf(np.concatenate([we, wy.reshape(D, L * D), wx], axis=1)),
            "bg": bf(np.random.standard_normal(D) * 0.3)}


def core(x, emb, Wg, bg):
    xf = f64(x)
    Wy = f64(Wg)[:, H:H + L * D].reshape(D, L, D)
    wx = f64(Wg)[:, -1]
    ctx = f64(emb) @ f64(Wg)[:, :H].T
    xq = mxq(xf[:, :T - 1, :], 2, "e4m3")
    wq = mxq(Wy, 2, "e4m3")
    lag = sum((xq[:, l:TM + l, :] @ wq[:, l, :].T) for l in range(L))
    return ctx[:, None, :] + lag + xf[:, L:, :] * wx + f64(bg)


def e4m3fn_bytes(y):
    return np.clip(np.asarray(y, np.float64), -448.0, 448.0).astype(np.float32).astype(ml_dtypes.float8_e4m3fn).view(np.uint8)


Y_SCALE = 210.0


def reference(x, emb, Wg, bg):
    out = core(x, emb, Wg, bg)
    return out, e4m3fn_bytes(out * Y_SCALE)

@@ -1,0 +1,254 @@
+from contextlib import ExitStack
+
+import concourse.mybir as mybir
+from concourse.masks import make_identity
+
+B, T, D, H, L = 128, 10, 1024, 128, 2
+TM = T - L
+Y_SCALE = 210.0
+FLOPS = 2 * B * TM * D * (L * D) + 2 * B * H * D
+
+F32 = mybir.dt.float32
+BF16 = mybir.dt.bfloat16
+U32 = mybir.dt.uint32
+U8 = mybir.dt.uint8
+FP8X4 = mybir.dt.float8_e4m3fn_x4
+FP8 = mybir.dt.float8_e4m3fn
+ALU = mybir.AluOpType
+ACT = mybir.ActivationFunctionType
+
+P = 128
+NH = 512
+WARM = 6
+
+
+def tile_npchangetransitionprior_pa_kernel(tc, x, emb, Wg, bg, out_0, out_1):
+    nc = tc.nc
+    with ExitStack() as ctx:
+        const = ctx.enter_context(tc.tile_pool(name="const", bufs=1))
+        stage = ctx.enter_context(tc.tile_pool(name="stage", bufs=4))
+        outs = ctx.enter_context(tc.tile_pool(name="outs", bufs=6))
+        psum = ctx.enter_context(tc.psum_pool(name="psum", bufs=1))
+
+        warm = const.tile([P, NH], BF16, name="warm")
+        nc.vector.memset(warm[:], 0.0)
+        ones = const.tile([P, P], BF16, name="ones")
+        nc.vector.memset(ones[:], 1.0)
+        tiny = const.tile([P, 2], F32, name="tiny")
+        nc.vector.memset(tiny[:], 0.0)
+        ident_f = const.tile([P, P], F32, name="ident_f")
+        make_identity(nc, ident_f[:])
+        ident_b = const.tile([P, P], BF16, name="ident_b")
+        make_identity(nc, ident_b[:])
+        bgz = const.tile([P, D], BF16, name="bgz")
+        nc.vector.memset(bgz[:], 0.0)
+
+        xs = [const.tile([P, D], BF16, name="x%d" % t) for t in range(T)]
+        raw = [[const.tile([P, D], BF16, name="w%d_%d" % (c, l)) for l in range(L)] for c in range(8)]
+        emb_sb = const.tile([P, H], BF16, name="emb_sb")
+        we_sb = const.tile([P, 8, H], BF16, name="we_sb")
+        wx_sb = const.tile([P, 8], BF16, name="wx_sb")
+
+        nc.scalar.activation(out=tiny[:, 1:2], in_=tiny[:, 0:1], func=ACT.Copy)
+
+        def load_x(t):
+            nc.sync.dma_start(out=xs[t][:], in_=x[:, t, :])
+
+        def load_w(c, l):
+            nc.sync.dma_start(out=raw[c][l][:], in_=Wg[c * P:(c + 1) * P, H + l * D:H + (l + 1) * D])
+
+        load_x(0)
+        load_x(1)
+        with nc.allow_non_contiguous_dma(reason="one weight of each row of Wg"):
+            nc.sync.dma_start(out=wx_sb[:], in_=Wg[:, 2176:2177].rearrange("(c p) o -> p (c o)", p=P))
+        nc.sync.dma_start(out=emb_sb[:], in_=emb[:, :])
+        nc.sync.dma_start(out=we_sb[:], in_=Wg[:, 0:H].rearrange("(c p) k -> p c k", p=P))
+        nc.sync.dma_start(out=bgz[0:1, :], in_=bg.unsqueeze(0))
+        load_x(2)
+        load_x(3)
+        for c in range(4):
+            load_w(c, 0)
+        load_x(4)
+        load_x(5)
+        for c in range(4):
+            load_w(c, 1)
+        for t in range(6, T):
+            load_x(t)
+        for c in range(4, 8):
+            load_w(c, 0)
+        for c in range(4, 8):
+            load_w(c, 1)
+
+        xq = [const.tile([P, 256], U32, name="xq%d" % t, align_bytes=64) for t in range(T - 1)]
+        xsc = [const.tile([P, 256], U8, name="xsc%d" % t, align_bytes=64) for t in range(T - 1)]
+        wq = [[const.tile([P, D], U32, name="wq%d_%d" % (l, g), align_bytes=64) for g in range(2)] for l in range(L)]
+        wsc = [[const.tile([P, D], U8, name="wsc%d_%d" % (l, g), align_bytes=64) for g in range(2)] for l in range(L)]
+        embT = const.tile([P, B], BF16, name="embT")
+        WeT = const.tile([P, D], BF16, name="WeT")
+        wxB = const.tile([P, D], F32, name="wxB")
+        vt = [[const.tile([P, 2, NH], F32, name="v%d_%d" % (h, j)) for j in range(4)] for h in range(2)]
+
+        def four_transposes(srcs):
+            tp = psum.tile([P, 4, P], F32, tag="tp", bufs=3, name="tp")
+            for i in range(2):
+                words, w0 = srcs[i]
+                for u in range(2):
+                    nc.tensor.transpose(tp[:, 2 * i + u, :], words[:, w0 + u:w0 + 256:2], ident_f[:])
+            return tp
+
+        def copy_quant(tp, codes, scales, on_vector):
+            grp = stage.tile([P, 1024], BF16, tag="grp", name="grp", align_bytes=64)
+            dst = grp[:].bitcast(F32).rearrange("p (i r u) -> p i r u", i=2, u=2)
+            src = tp[:].rearrange("p (i u) r -> p i r u", u=2)
+            if on_vector:
+                nc.vector.tensor_copy(out=dst, in_=src)
+            else:
+                nc.scalar.copy(out=dst, in_=src)
+            nc.vector.quantize_mx(out=codes.bitcast(FP8X4), scales=scales, in_=grp[:])
+
+        def unit(spec):
+            if spec[0] == "x":
+                t = spec[1]
+                words = xs[t][:].bitcast(F32)
+                tp = four_transposes([(words, 0), (words, 256)])
+                copy_quant(tp, xq[t][:], xsc[t][:], t in (1, 3))
+            else:
+                l, g, cp = spec[1], spec[2], spec[3]
+                tp = four_transposes([(raw[2 * cp + ci][l][:].bitcast(F32), 256 * g) for ci in range(2)])
+                cols = slice(cp * 256, (cp + 1) * 256)
+                copy_quant(tp, wq[l][g][:, cols], wsc[l][g][:, cols], False)
+
+        def mm(acc, t, h, l, g):
+            bcols = slice(g * P, (g + 1) * P)
+            dcols = slice(h * NH, (h + 1) * NH)
+            nc.tensor.matmul_mx(
+                out=acc[:],
+                lhsT=xq[t + l][:, bcols].bitcast(FP8X4),
+                lhsT_scale=xsc[t + l][:, bcols],
+                rhs=wq[l][g][:, dcols].bitcast(FP8X4),
+                rhs_scale=wsc[l][g][:, dcols],
+                start=(l == 0 and g == 0),
+                stop=(l == 1 and g == 1),
+            )
+
+        def new_acc():
+            return psum.tile([P, NH], F32, tag="acc", bufs=4, name="acc")
+
+        def dummies(n):
+            wps = psum.tile([P, NH], F32, tag="acc", bufs=4, name="wps")
+            for i in range(n):
+                nc.tensor.matmul(wps[:], lhsT=ones[:], rhs=warm[:], start=True, stop=True)
+
+        def small_transposes():
+            tpe = psum.tile([P, B], BF16, tag="tp", bufs=3, name="tpe")
+            nc.tensor.transpose(tpe[:], emb_sb[:], ident_b[:])
+            nc.scalar.copy(out=embT[:], in_=tpe[:])
+            tpw = psum.tile([P, D], BF16, tag="tp", bufs=3, name="tpw")
+            for c in range(8):
+                nc.tensor.transpose(tpw[:, c * P:(c + 1) * P], we_sb[:, c, :], ident_b[:])
+            nc.scalar.copy(out=WeT[:], in_=tpw[:])
+
+        def wx_spread():
+            for h in range(2):
+                wxp = psum.tile([P, NH], F32, tag="acc", bufs=4, name="wxp")
+                for ci in range(4):
+                    c = 4 * h + ci
+                    nc.tensor.matmul(
+                        wxp[:, ci * P:(ci + 1) * P],
+                        lhsT=wx_sb[:, c:c + 1].to_broadcast([P, P]),
+                        rhs=ident_b[:],
+                        start=True,
+                        stop=True,
+                    )
+                if h == 0:
+                    nc.vector.tensor_copy(out=wxB[:, h * NH:(h + 1) * NH], in_=wxp[:])
+                else:
+                    nc.scalar.copy(out=wxB[:, h * NH:(h + 1) * NH], in_=wxp[:])
+            for h in range(2):
+                dcols = slice(h * NH, (h + 1) * NH)
+                for t in range(TM):
+                    nc.gpsimd.tensor_tensor(
+                        out=vt[h][t // 2][:, t % 2, :],
+                        in0=xs[t + 2][:, dcols],
+                        in1=wxB[:, dcols],
+                        op=ALU.mult,
+                    )
+
+        def ctx_bias(h):
+            dcols = slice(h * NH, (h + 1) * NH)
+            cps = psum.tile([P, NH], F32, tag="cb", bufs=1, name="cps")
+            nc.tensor.matmul(cps[:], lhsT=embT[:], rhs=WeT[:, dcols], start=True, stop=False)
+            nc.tensor.matmul(cps[:], lhsT=ones[:], rhs=bgz[:, dcols], start=False, stop=True)
+            for j in range(4):
+                nc.vector.tensor_tensor(
+                    out=vt[h][j][:],
+                    in0=vt[h][j][:],
+                    in1=cps[:].unsqueeze(1).to_broadcast([P, 2, NH]),
+                    op=ALU.add,
+                )
+
+        o8s = {}
+
+        def epilogue(acc, t, h):
+            dcols = slice(h * NH, (h + 1) * NH)
+            if t % 4 == 0:
+                o8s[h] = outs.tile([P, 4, NH], FP8, tag="o8", bufs=2, name="o8")
+            o8 = o8s[h]
+            o = outs.tile([P, NH], F32, tag="o", name="o")
+            nc.vector.tensor_tensor(out=o[:], in0=acc[:], in1=vt[h][t // 2][:, t % 2, :], op=ALU.add)
+            nc.scalar.activation(out=o8[:, t % 4, :], in_=o[:], func=ACT.Copy, scale=Y_SCALE, saturate=False)
+            nc.sync.dma_start(out=out_0[:, t, dcols], in_=o[:])
+            if t % 4 == 3:
+                nc.sync.dma_start(out=out_1[:, t - 3:t + 1, dcols], in_=o8[:].bitcast(U8))
+
+        lg = [(l, g) for l in range(L) for g in range(2)]
+        units = [("x", t) for t in range(4)]
+        units += [("w", 0, g, cp) for g in range(2) for cp in range(2)]
+        units += [("x", 4)]
+        units += [("w", 1, g, cp) for g in range(2) for cp in range(2)]
+        units += [("x", t) for t in range(5, 9)]
+        units += [("w", l, g, cp) for (l, g) in lg for cp in (2, 3)]
+        truns = [units[i:i + 2] for i in range(0, len(units), 2)]
+
+        accs = {}
+
+        def mm_run(i):
+            h, k = i // 8, i % 8
+            if h == 0 and k < 4:
+                l, g = lg[k]
+                for t in range(4):
+                    if k == 0:
+                        accs[t] = new_acc()
+                    mm(accs[t], t, h, l, g)
+                if k == 3:
+                    for t in range(4):
+                        epilogue(accs[t], t, h)
+            else:
+                acc = new_acc()
+                for (l, g) in lg:
+                    mm(acc, k, h, l, g)
+                epilogue(acc, k, h)
+
+        def t_run(i):
+            for spec in truns[i]:
+                unit(spec)
+
+        AHEAD = 6
+        with tc.manual_schedule(engines={mybir.EngineType.PE}):
+            dummies(WARM)
+            t_run(0)
+            t_run(1)
+            wx_spread()
+            small_transposes()
+            t_run(2)
+            ctx_bias(0)
+            t_run(3)
+            dummies(2)
+            t_run(4)
+            t_run(5)
+            for i in range(16):
+                mm_run(i)
+                if i + AHEAD < len(truns):
+                    t_run(i + AHEAD)
+                if i == 4:
+                    ctx_bias(1)

@@ -19,7 +19,6 @@ ACT = mybir.ActivationFunctionType
 
 P = 128
 NH = 512
-WARM = 6
 
 
 def tile_npchangetransitionprior_pa_kernel(tc, x, emb, Wg, bg, out_0, out_1):
@@ -29,6 +28,7 @@ def tile_npchangetransitionprior_pa_kernel(tc, x, emb, Wg, bg, out_0, out_1):
         stage = ctx.enter_context(tc.tile_pool(name="stage", bufs=4))
         outs = ctx.enter_context(tc.tile_pool(name="outs", bufs=6))
         psum = ctx.enter_context(tc.psum_pool(name="psum", bufs=1))
+        ctx.enter_context(tc.manual_schedule())
 
         warm = const.tile([P, NH], BF16, name="warm")
         nc.vector.memset(warm[:], 0.0)
@@ -58,21 +58,18 @@ def tile_npchangetransitionprior_pa_kernel(tc, x, emb, Wg, bg, out_0, out_1):
             nc.sync.dma_start(out=raw[c][l][:], in_=Wg[c * P:(c + 1) * P, H + l * D:H + (l + 1) * D])
 
         load_x(0)
-        load_x(1)
         with nc.allow_non_contiguous_dma(reason="one weight of each row of Wg"):
             nc.sync.dma_start(out=wx_sb[:], in_=Wg[:, 2176:2177].rearrange("(c p) o -> p (c o)", p=P))
         nc.sync.dma_start(out=emb_sb[:], in_=emb[:, :])
         nc.sync.dma_start(out=we_sb[:], in_=Wg[:, 0:H].rearrange("(c p) k -> p c k", p=P))
         nc.sync.dma_start(out=bgz[0:1, :], in_=bg.unsqueeze(0))
-        load_x(2)
-        load_x(3)
+        for t in range(1, 5):
+            load_x(t)
         for c in range(4):
             load_w(c, 0)
-        load_x(4)
-        load_x(5)
         for c in range(4):
             load_w(c, 1)
-        for t in range(6, T):
+        for t in range(5, T):
             load_x(t)
         for c in range(4, 8):
             load_w(c, 0)
@@ -89,7 +86,7 @@ def tile_npchangetransitionprior_pa_kernel(tc, x, emb, Wg, bg, out_0, out_1):
         vt = [[const.tile([P, 2, NH], F32, name="v%d_%d" % (h, j)) for j in range(4)] for h in range(2)]
 
         def four_transposes(srcs):
-            tp = psum.tile([P, 4, P], F32, tag="tp", bufs=3, name="tp")
+            tp = psum.tile([P, 4, P], F32, tag="tp", bufs=4, name="tp")
             for i in range(2):
                 words, w0 = srcs[i]
                 for u in range(2):
@@ -111,7 +108,7 @@ def tile_npchangetransitionprior_pa_kernel(tc, x, emb, Wg, bg, out_0, out_1):
                 t = spec[1]
                 words = xs[t][:].bitcast(F32)
                 tp = four_transposes([(words, 0), (words, 256)])
-                copy_quant(tp, xq[t][:], xsc[t][:], t in (1, 3))
+                copy_quant(tp, xq[t][:], xsc[t][:], False)
             else:
                 l, g, cp = spec[1], spec[2], spec[3]
                 tp = four_transposes([(raw[2 * cp + ci][l][:].bitcast(F32), 256 * g) for ci in range(2)])
@@ -132,25 +129,25 @@ def tile_npchangetransitionprior_pa_kernel(tc, x, emb, Wg, bg, out_0, out_1):
             )
 
         def new_acc():
-            return psum.tile([P, NH], F32, tag="acc", bufs=4, name="acc")
+            return psum.tile([P, NH], F32, tag="acc", bufs=3, name="acc")
 
         def dummies(n):
-            wps = psum.tile([P, NH], F32, tag="acc", bufs=4, name="wps")
+            wps = psum.tile([P, NH], F32, tag="acc", bufs=3, name="wps")
             for i in range(n):
                 nc.tensor.matmul(wps[:], lhsT=ones[:], rhs=warm[:], start=True, stop=True)
 
         def small_transposes():
-            tpe = psum.tile([P, B], BF16, tag="tp", bufs=3, name="tpe")
+            tpe = psum.tile([P, B], BF16, tag="tp", bufs=4, name="tpe")
             nc.tensor.transpose(tpe[:], emb_sb[:], ident_b[:])
             nc.scalar.copy(out=embT[:], in_=tpe[:])
-            tpw = psum.tile([P, D], BF16, tag="tp", bufs=3, name="tpw")
+            tpw = psum.tile([P, D], BF16, tag="tp", bufs=4, name="tpw")
             for c in range(8):
                 nc.tensor.transpose(tpw[:, c * P:(c + 1) * P], we_sb[:, c, :], ident_b[:])
             nc.scalar.copy(out=WeT[:], in_=tpw[:])
 
         def wx_spread():
             for h in range(2):
-                wxp = psum.tile([P, NH], F32, tag="acc", bufs=4, name="wxp")
+                wxp = psum.tile([P, NH], F32, tag="acc", bufs=3, name="wxp")
                 for ci in range(4):
                     c = 4 * h + ci
                     nc.tensor.matmul(
@@ -174,81 +171,113 @@ def tile_npchangetransitionprior_pa_kernel(tc, x, emb, Wg, bg, out_0, out_1):
                         op=ALU.mult,
                     )
 
+        cbank = {}
+
         def ctx_bias(h):
             dcols = slice(h * NH, (h + 1) * NH)
             cps = psum.tile([P, NH], F32, tag="cb", bufs=1, name="cps")
             nc.tensor.matmul(cps[:], lhsT=embT[:], rhs=WeT[:, dcols], start=True, stop=False)
             nc.tensor.matmul(cps[:], lhsT=ones[:], rhs=bgz[:, dcols], start=False, stop=True)
-            for j in range(4):
-                nc.vector.tensor_tensor(
-                    out=vt[h][j][:],
-                    in0=vt[h][j][:],
-                    in1=cps[:].unsqueeze(1).to_broadcast([P, 2, NH]),
-                    op=ALU.add,
-                )
+            cbank[h] = cps
+
+        def side_add(h, j):
+            nc.vector.tensor_tensor(
+                out=vt[h][j][:],
+                in0=vt[h][j][:],
+                in1=cbank[h][:].unsqueeze(1).to_broadcast([P, 2, NH]),
+                op=ALU.add,
+            )
 
         o8s = {}
+        accs = {}
+        res = {}
 
-        def epilogue(acc, t, h):
+        def add(h, t):
+            o = outs.tile([P, NH], F32, tag="o", name="o")
+            nc.vector.tensor_tensor(out=o[:], in0=accs[(h, t)][:], in1=vt[h][t // 2][:, t % 2, :], op=ALU.add)
+            res[(h, t)] = o
+
+        def cast(h, t):
             dcols = slice(h * NH, (h + 1) * NH)
             if t % 4 == 0:
                 o8s[h] = outs.tile([P, 4, NH], FP8, tag="o8", bufs=2, name="o8")
             o8 = o8s[h]
-            o = outs.tile([P, NH], F32, tag="o", name="o")
-            nc.vector.tensor_tensor(out=o[:], in0=acc[:], in1=vt[h][t // 2][:, t % 2, :], op=ALU.add)
+            o = res[(h, t)]
             nc.scalar.activation(out=o8[:, t % 4, :], in_=o[:], func=ACT.Copy, scale=Y_SCALE, saturate=False)
             nc.sync.dma_start(out=out_0[:, t, dcols], in_=o[:])
             if t % 4 == 3:
                 nc.sync.dma_start(out=out_1[:, t - 3:t + 1, dcols], in_=o8[:].bitcast(U8))
 
         lg = [(l, g) for l in range(L) for g in range(2)]
-        units = [("x", t) for t in range(4)]
-        units += [("w", 0, g, cp) for g in range(2) for cp in range(2)]
-        units += [("x", 4)]
-        units += [("w", 1, g, cp) for g in range(2) for cp in range(2)]
-        units += [("x", t) for t in range(5, 9)]
-        units += [("w", l, g, cp) for (l, g) in lg for cp in (2, 3)]
-        truns = [units[i:i + 2] for i in range(0, len(units), 2)]
 
-        accs = {}
+        def mms(h, t):
+            acc = new_acc()
+            for (l, g) in lg:
+                mm(acc, t, h, l, g)
+            accs[(h, t)] = acc
 
-        def mm_run(i):
-            h, k = i // 8, i % 8
-            if h == 0 and k < 4:
-                l, g = lg[k]
-                for t in range(4):
-                    if k == 0:
-                        accs[t] = new_acc()
-                    mm(accs[t], t, h, l, g)
-                if k == 3:
-                    for t in range(4):
-                        epilogue(accs[t], t, h)
-            else:
-                acc = new_acc()
-                for (l, g) in lg:
-                    mm(acc, k, h, l, g)
-                epilogue(acc, k, h)
+        def x_units(ts):
+            for t in ts:
+                unit(("x", t))
 
-        def t_run(i):
-            for spec in truns[i]:
-                unit(spec)
+        def w_units(l, g, h):
+            for cp in (2 * h, 2 * h + 1):
+                unit(("w", l, g, cp))
 
-        AHEAD = 6
-        with tc.manual_schedule(engines={mybir.EngineType.PE}):
-            dummies(WARM)
-            t_run(0)
-            t_run(1)
-            wx_spread()
-            small_transposes()
-            t_run(2)
-            ctx_bias(0)
-            t_run(3)
-            dummies(2)
-            t_run(4)
-            t_run(5)
-            for i in range(16):
-                mm_run(i)
-                if i + AHEAD < len(truns):
-                    t_run(i + AHEAD)
-                if i == 4:
-                    ctx_bias(1)
+        dummies(4)
+        x_units([0])
+        wx_spread()
+        small_transposes()
+        x_units([1, 2])
+        ctx_bias(0)
+        x_units([3, 4])
+        dummies(2)
+        w_units(0, 0, 0)
+        side_add(0, 0)
+        w_units(0, 1, 0)
+        dummies(2)
+        w_units(1, 0, 0)
+        side_add(0, 1)
+        w_units(1, 1, 0)
+        dummies(2)
+        x_units([5, 6])
+        mms(0, 0)
+        mms(0, 1)
+        add(0, 0)
+        add(0, 1)
+        x_units([7, 8])
+        side_add(0, 2)
+        cast(0, 0)
+        cast(0, 1)
+        mms(0, 2)
+        mms(0, 3)
+        add(0, 2)
+        add(0, 3)
+        side_add(0, 3)
+        w_units(0, 0, 1)
+        w_units(0, 1, 1)
+        cast(0, 2)
+        cast(0, 3)
+        mms(0, 4)
+        mms(0, 5)
+        ctx_bias(1)
+        add(0, 4)
+        add(0, 5)
+        w_units(1, 0, 1)
+        w_units(1, 1, 1)
+        side_add(1, 0)
+        cast(0, 4)
+        cast(0, 5)
+        mms(0, 6)
+        mms(0, 7)
+        add(0, 6)
+        add(0, 7)
+        side_add(1, 1)
+        cast(0, 6)
+        cast(0, 7)
+        for t in range(TM):
+            mms(1, t)
+            if t in (1, 3):
+                side_add(1, (t + 3) // 2)
+            add(1, t)
+            cast(1, t)

@@ -207,6 +207,36 @@ def tile_npchangetransitionprior_pa_kernel(tc, x, emb, Wg, bg, out_0, out_1):
             nc.sync.dma_start(out=out_0[:, t, dcols], in_=o[:])
             if t % 4 == 3:
                 nc.sync.dma_start(out=out_1[:, t - 3:t + 1, dcols], in_=o8[:].bitcast(U8))
+            if h == 1 and t == TM - 2:
+                nc.sync.dma_start(out=out_1[:, t - 2:t + 1, dcols], in_=o8[:, 0:3, :].bitcast(U8))
+
+        def last_group():
+            h, t = 1, TM - 1
+            NQ = NH // 2
+            halves = []
+            for q in range(2):
+                acc = psum.tile([P, NQ], F32, tag="acc", bufs=3, name="accq")
+                for (l, g) in lg:
+                    bcols = slice(g * P, (g + 1) * P)
+                    dq = slice(h * NH + q * NQ, h * NH + (q + 1) * NQ)
+                    nc.tensor.matmul_mx(
+                        out=acc[:],
+                        lhsT=xq[t + l][:, bcols].bitcast(FP8X4),
+                        lhsT_scale=xsc[t + l][:, bcols],
+                        rhs=wq[l][g][:, dq].bitcast(FP8X4),
+                        rhs_scale=wsc[l][g][:, dq],
+                        start=(l == 0 and g == 0),
+                        stop=(l == 1 and g == 1),
+                    )
+                halves.append(acc)
+            for q in range(2):
+                dq = slice(h * NH + q * NQ, h * NH + (q + 1) * NQ)
+                o = outs.tile([P, NQ], F32, tag="oq", bufs=2, name="oq")
+                nc.vector.tensor_tensor(out=o[:], in0=halves[q][:], in1=vt[h][t // 2][:, t % 2, q * NQ:(q + 1) * NQ], op=ALU.add)
+                o8 = outs.tile([P, NQ], FP8, tag="o8q", bufs=2, name="o8q")
+                nc.scalar.activation(out=o8[:], in_=o[:], func=ACT.Copy, scale=Y_SCALE, saturate=False)
+                nc.sync.dma_start(out=out_0[:, t, dq], in_=o[:])
+                nc.sync.dma_start(out=out_1[:, t, dq], in_=o8[:].bitcast(U8))
 
         lg = [(l, g) for l in range(L) for g in range(2)]
 
@@ -275,9 +305,10 @@ def tile_npchangetransitionprior_pa_kernel(tc, x, emb, Wg, bg, out_0, out_1):
         side_add(1, 1)
         cast(0, 6)
         cast(0, 7)
-        for t in range(TM):
+        for t in range(TM - 1):
             mms(1, t)
             if t in (1, 3):
                 side_add(1, (t + 3) // 2)
             add(1, t)
             cast(1, t)
+        last_group()

@@ -18,14 +18,17 @@ ALU = mybir.AluOpType
 ACT = mybir.ActivationFunctionType
 
 P = 128
+LOADS = "x0 x1 e c0 c1 x2 x3 x4 x5 x6 x7 x8 x9 c2 c3 c4 c5 c6 c7"
+NQ = 256
 NH = 512
+FW = H + L * D
 
 
 def tile_npchangetransitionprior_pa_kernel(tc, x, emb, Wg, bg, out_0, out_1):
     nc = tc.nc
     with ExitStack() as ctx:
         const = ctx.enter_context(tc.tile_pool(name="const", bufs=1))
-        stage = ctx.enter_context(tc.tile_pool(name="stage", bufs=4))
+        stage = ctx.enter_context(tc.tile_pool(name="stage", bufs=2))
         outs = ctx.enter_context(tc.tile_pool(name="outs", bufs=6))
         psum = ctx.enter_context(tc.psum_pool(name="psum", bufs=1))
         ctx.enter_context(tc.manual_schedule())
@@ -43,272 +46,267 @@ def tile_npchangetransitionprior_pa_kernel(tc, x, emb, Wg, bg, out_0, out_1):
         bgz = const.tile([P, D], BF16, name="bgz")
         nc.vector.memset(bgz[:], 0.0)
 
-        xs = [const.tile([P, D], BF16, name="x%d" % t) for t in range(T)]
-        raw = [[const.tile([P, D], BF16, name="w%d_%d" % (c, l)) for l in range(L)] for c in range(8)]
+        xp = [const.tile([P, 2, D], BF16, name="xp%d" % j) for j in range(T // 2)]
+        wt = [const.tile([P, FW], BF16, name="wt%d" % c) for c in range(8)]
         emb_sb = const.tile([P, H], BF16, name="emb_sb")
-        we_sb = const.tile([P, 8, H], BF16, name="we_sb")
         wx_sb = const.tile([P, 8], BF16, name="wx_sb")
 
         nc.scalar.activation(out=tiny[:, 1:2], in_=tiny[:, 0:1], func=ACT.Copy)
 
-        def load_x(t):
-            nc.sync.dma_start(out=xs[t][:], in_=x[:, t, :])
+        for s in LOADS.split():
+            if s == "e":
+                with nc.allow_non_contiguous_dma(reason="one weight of each row of Wg"):
+                    nc.sync.dma_start(out=wx_sb[:], in_=Wg[:, FW:FW + 1].rearrange("(c p) o -> p (c o)", p=P))
+                nc.sync.dma_start(out=emb_sb[:], in_=emb[:, :])
+                nc.sync.dma_start(out=bgz[0:1, :], in_=bg.unsqueeze(0))
+            elif s[0] == "x":
+                t = int(s[1])
+                nc.sync.dma_start(out=xp[t // 2][:, t % 2, :], in_=x[:, t, :])
+            else:
+                c = int(s[1])
+                nc.sync.dma_start(out=wt[c][:], in_=Wg[c * P:(c + 1) * P, 0:FW])
 
-        def load_w(c, l):
-            nc.sync.dma_start(out=raw[c][l][:], in_=Wg[c * P:(c + 1) * P, H + l * D:H + (l + 1) * D])
-
-        load_x(0)
-        with nc.allow_non_contiguous_dma(reason="one weight of each row of Wg"):
-            nc.sync.dma_start(out=wx_sb[:], in_=Wg[:, 2176:2177].rearrange("(c p) o -> p (c o)", p=P))
-        nc.sync.dma_start(out=emb_sb[:], in_=emb[:, :])
-        nc.sync.dma_start(out=we_sb[:], in_=Wg[:, 0:H].rearrange("(c p) k -> p c k", p=P))
-        nc.sync.dma_start(out=bgz[0:1, :], in_=bg.unsqueeze(0))
-        for t in range(1, 5):
-            load_x(t)
-        for c in range(4):
-            load_w(c, 0)
-        for c in range(4):
-            load_w(c, 1)
-        for t in range(5, T):
-            load_x(t)
-        for c in range(4, 8):
-            load_w(c, 0)
-        for c in range(4, 8):
-            load_w(c, 1)
-
-        xq = [const.tile([P, 256], U32, name="xq%d" % t, align_bytes=64) for t in range(T - 1)]
-        xsc = [const.tile([P, 256], U8, name="xsc%d" % t, align_bytes=64) for t in range(T - 1)]
-        wq = [[const.tile([P, D], U32, name="wq%d_%d" % (l, g), align_bytes=64) for g in range(2)] for l in range(L)]
-        wsc = [[const.tile([P, D], U8, name="wsc%d_%d" % (l, g), align_bytes=64) for g in range(2)] for l in range(L)]
+        xq = [const.tile([P, 2, 256], U32, name="xq%d" % j, align_bytes=64) for j in range(T // 2)]
+        xsc = [const.tile([P, 2, 256], U8, name="xsc%d" % j, align_bytes=64) for j in range(T // 2)]
+        wq = [const.tile([P, 4, NQ], U32, name="wq%d" % cp, align_bytes=64) for cp in range(4)]
+        wsc = [const.tile([P, 4, NQ], U8, name="wsc%d" % cp, align_bytes=64) for cp in range(4)]
         embT = const.tile([P, B], BF16, name="embT")
         WeT = const.tile([P, D], BF16, name="WeT")
         wxB = const.tile([P, D], F32, name="wxB")
-        vt = [[const.tile([P, 2, NH], F32, name="v%d_%d" % (h, j)) for j in range(4)] for h in range(2)]
+        vt = [[const.tile([P, 2, NQ], F32, name="v%d_%d" % (cp, j)) for j in range(4)] for cp in range(4)]
 
-        def four_transposes(srcs):
+        def cp_eng(eng, out, in_):
+            if eng == "v":
+                nc.vector.tensor_copy(out=out, in_=in_)
+            else:
+                nc.scalar.copy(out=out, in_=in_)
+
+        tps = {}
+        grps = {}
+
+        def four(words):
             tp = psum.tile([P, 4, P], F32, tag="tp", bufs=4, name="tp")
-            for i in range(2):
-                words, w0 = srcs[i]
+            for g in range(2):
                 for u in range(2):
-                    nc.tensor.transpose(tp[:, 2 * i + u, :], words[:, w0 + u:w0 + 256:2], ident_f[:])
+                    nc.tensor.transpose(tp[:, 2 * g + u, :], words[:, 256 * g + u:256 * (g + 1):2], ident_f[:])
             return tp
 
-        def copy_quant(tp, codes, scales, on_vector):
-            grp = stage.tile([P, 1024], BF16, tag="grp", name="grp", align_bytes=64)
-            dst = grp[:].bitcast(F32).rearrange("p (i r u) -> p i r u", i=2, u=2)
-            src = tp[:].rearrange("p (i u) r -> p i r u", u=2)
-            if on_vector:
-                nc.vector.tensor_copy(out=dst, in_=src)
-            else:
-                nc.scalar.copy(out=dst, in_=src)
-            nc.vector.quantize_mx(out=codes.bitcast(FP8X4), scales=scales, in_=grp[:])
+        def TX(t):
+            tps[("x", t)] = four(xp[t // 2][:, t % 2, :].bitcast(F32))
 
-        def unit(spec):
-            if spec[0] == "x":
-                t = spec[1]
-                words = xs[t][:].bitcast(F32)
-                tp = four_transposes([(words, 0), (words, 256)])
-                copy_quant(tp, xq[t][:], xsc[t][:], False)
-            else:
-                l, g, cp = spec[1], spec[2], spec[3]
-                tp = four_transposes([(raw[2 * cp + ci][l][:].bitcast(F32), 256 * g) for ci in range(2)])
-                cols = slice(cp * 256, (cp + 1) * 256)
-                copy_quant(tp, wq[l][g][:, cols], wsc[l][g][:, cols], False)
+        def TW(c, l):
+            tps[("w", c, l)] = four(wt[c][:, H + l * D:H + (l + 1) * D].bitcast(F32))
 
-        def mm(acc, t, h, l, g):
-            bcols = slice(g * P, (g + 1) * P)
-            dcols = slice(h * NH, (h + 1) * NH)
-            nc.tensor.matmul_mx(
-                out=acc[:],
-                lhsT=xq[t + l][:, bcols].bitcast(FP8X4),
-                lhsT_scale=xsc[t + l][:, bcols],
-                rhs=wq[l][g][:, dcols].bitcast(FP8X4),
-                rhs_scale=wsc[l][g][:, dcols],
-                start=(l == 0 and g == 0),
-                stop=(l == 1 and g == 1),
+        def CX(t, eng="s"):
+            if t % 2 == 0:
+                grps[("x", t // 2)] = stage.tile([P, 2, 1024], BF16, tag="grpx", bufs=3, name="grpx", align_bytes=64)
+            dst = grps[("x", t // 2)][:, t % 2, :].bitcast(F32).rearrange("p (g r u) -> p g r u", g=2, u=2)
+            cp_eng(eng, dst, tps[("x", t)][:].rearrange("p (g u) r -> p g r u", u=2))
+
+        def CW(c, l, eng="s"):
+            cp, ci = c // 2, c % 2
+            if ci == 0:
+                grps[(cp, l)] = stage.tile([P, 2, 2, 512], BF16, tag="grpw", bufs=4, name="grpw", align_bytes=64)
+            dst = grps[(cp, l)][:, :, ci, :].bitcast(F32).rearrange("p g (r u) -> p g r u", u=2)
+            cp_eng(eng, dst, tps[("w", c, l)][:].rearrange("p (g u) r -> p g r u", u=2))
+
+        def QX(t):
+            nc.vector.quantize_mx(out=xq[t // 2][:, t % 2, :].bitcast(FP8X4), scales=xsc[t // 2][:, t % 2, :], in_=grps[("x", t // 2)][:, t % 2, :])
+
+        def QW(cp, l):
+            nc.vector.quantize_mx(
+                out=wq[cp][:, 2 * l:2 * l + 2, :].rearrange("p a r -> p (a r)").bitcast(FP8X4),
+                scales=wsc[cp][:, 2 * l:2 * l + 2, :].rearrange("p a r -> p (a r)"),
+                in_=grps[(cp, l)][:].rearrange("p g c r -> p (g c r)"),
             )
 
-        def new_acc():
-            return psum.tile([P, NH], F32, tag="acc", bufs=3, name="acc")
+        def group(bank, slot, t, cp):
+            for a in range(4):
+                l, g = a // 2, a % 2
+                s = t + l
+                bcols = slice(g * P, (g + 1) * P)
+                nc.tensor.matmul_mx(
+                    out=bank[:, slot * NQ:(slot + 1) * NQ],
+                    lhsT=xq[s // 2][:, s % 2, bcols].bitcast(FP8X4),
+                    lhsT_scale=xsc[s // 2][:, s % 2, bcols],
+                    rhs=wq[cp][:, a, :].bitcast(FP8X4),
+                    rhs_scale=wsc[cp][:, a, :],
+                    start=(a == 0),
+                    stop=(a == 3),
+                )
 
         def dummies(n):
             wps = psum.tile([P, NH], F32, tag="acc", bufs=3, name="wps")
             for i in range(n):
                 nc.tensor.matmul(wps[:], lhsT=ones[:], rhs=warm[:], start=True, stop=True)
 
-        def small_transposes():
+        def emb_transpose():
             tpe = psum.tile([P, B], BF16, tag="tp", bufs=4, name="tpe")
             nc.tensor.transpose(tpe[:], emb_sb[:], ident_b[:])
             nc.scalar.copy(out=embT[:], in_=tpe[:])
-            tpw = psum.tile([P, D], BF16, tag="tp", bufs=4, name="tpw")
-            for c in range(8):
-                nc.tensor.transpose(tpw[:, c * P:(c + 1) * P], we_sb[:, c, :], ident_b[:])
-            nc.scalar.copy(out=WeT[:], in_=tpw[:])
 
-        def wx_spread():
-            for h in range(2):
-                wxp = psum.tile([P, NH], F32, tag="acc", bufs=3, name="wxp")
-                for ci in range(4):
-                    c = 4 * h + ci
-                    nc.tensor.matmul(
-                        wxp[:, ci * P:(ci + 1) * P],
-                        lhsT=wx_sb[:, c:c + 1].to_broadcast([P, P]),
-                        rhs=ident_b[:],
-                        start=True,
-                        stop=True,
-                    )
-                if h == 0:
-                    nc.vector.tensor_copy(out=wxB[:, h * NH:(h + 1) * NH], in_=wxp[:])
-                else:
-                    nc.scalar.copy(out=wxB[:, h * NH:(h + 1) * NH], in_=wxp[:])
-            for h in range(2):
-                dcols = slice(h * NH, (h + 1) * NH)
-                for t in range(TM):
-                    nc.gpsimd.tensor_tensor(
-                        out=vt[h][t // 2][:, t % 2, :],
-                        in0=xs[t + 2][:, dcols],
-                        in1=wxB[:, dcols],
-                        op=ALU.mult,
-                    )
+        def wx_matmuls(h):
+            wxp = psum.tile([P, NH], F32, tag="acc", bufs=3, name="wxp")
+            for ci in range(4):
+                c = 4 * h + ci
+                nc.tensor.matmul(wxp[:, ci * P:(ci + 1) * P], lhsT=wx_sb[:, c:c + 1].to_broadcast([P, P]), rhs=ident_b[:], start=True, stop=True)
+            return wxp
+
+        def wx_copy(h, wxp):
+            nc.scalar.copy(out=wxB[:, h * NH:(h + 1) * NH], in_=wxp[:])
 
         cbank = {}
 
-        def ctx_bias(h):
-            dcols = slice(h * NH, (h + 1) * NH)
-            cps = psum.tile([P, NH], F32, tag="cb", bufs=1, name="cps")
-            nc.tensor.matmul(cps[:], lhsT=embT[:], rhs=WeT[:, dcols], start=True, stop=False)
-            nc.tensor.matmul(cps[:], lhsT=ones[:], rhs=bgz[:, dcols], start=False, stop=True)
-            cbank[h] = cps
+        def WE(cp):
+            dcols = slice(cp * NQ, (cp + 1) * NQ)
+            tpw = psum.tile([P, NQ], BF16, tag="tp", bufs=4, name="tpw")
+            for ci in range(2):
+                nc.tensor.transpose(tpw[:, ci * P:(ci + 1) * P], wt[2 * cp + ci][:, 0:H], ident_b[:])
+            nc.scalar.copy(out=WeT[:, dcols], in_=tpw[:])
 
-        def side_add(h, j):
+        def CB(cp):
+            dcols = slice(cp * NQ, (cp + 1) * NQ)
+            if cp < 3:
+                cbank[min(cp, 2)] = psum.tile([P, NH], F32, tag="cb", bufs=1, name="cps")
+            cps = cbank[min(cp, 2)][:, (cp // 3) * NQ:(cp // 3 + 1) * NQ]
+            nc.tensor.matmul(cps, lhsT=embT[:], rhs=WeT[:, dcols], start=True, stop=False)
+            nc.tensor.matmul(cps, lhsT=ones[:], rhs=bgz[:, dcols], start=False, stop=True)
+
+        junk = const.tile([P, 8], F32, name="junk")
+
+        def wait_for(i, ap):
+            nc.gpsimd.tensor_copy(out=junk[:, i:i + 1], in_=ap)
+
+        def PR(j, cp, eng="g"):
+            dcols = slice(cp * NQ, (cp + 1) * NQ)
+            e = nc.gpsimd if eng == "g" else nc.vector
+            e.tensor_tensor(out=vt[cp][j][:], in0=xp[j + 1][:, :, dcols], in1=wxB[:, dcols].unsqueeze(1).to_broadcast([P, 2, NQ]), op=ALU.mult)
+
+        def SA(j, cp):
+            cps = cbank[min(cp, 2)][:, (cp // 3) * NQ:(cp // 3 + 1) * NQ]
+            nc.vector.tensor_tensor(out=vt[cp][j][:], in0=vt[cp][j][:], in1=cps.unsqueeze(1).to_broadcast([P, 2, NQ]), op=ALU.add)
+
+        banks = {}
+        res = {}
+        o8s = {}
+
+        def M(j, cp):
+            bank = psum.tile([P, NH], F32, tag="acc", bufs=3, name="acc")
+            group(bank, 0, 2 * j, cp)
+            group(bank, 1, 2 * j + 1, cp)
+            banks[(j, cp)] = bank
+
+        def A(j, cp):
+            h, q = cp // 2, cp % 2
+            if q == 0:
+                res[(j, h)] = outs.tile([P, 2, NH], F32, tag="o", bufs=6, name="o")
             nc.vector.tensor_tensor(
-                out=vt[h][j][:],
-                in0=vt[h][j][:],
-                in1=cbank[h][:].unsqueeze(1).to_broadcast([P, 2, NH]),
+                out=res[(j, h)][:, :, q * NQ:(q + 1) * NQ],
+                in0=banks[(j, cp)][:].rearrange("p (s n) -> p s n", s=2),
+                in1=vt[cp][j][:],
                 op=ALU.add,
             )
+            if q == 1:
+                nc.sync.dma_start(out=out_0[:, 2 * j:2 * j + 2, h * NH:(h + 1) * NH], in_=res[(j, h)][:])
 
-        o8s = {}
-        accs = {}
-        res = {}
-
-        def add(h, t):
-            o = outs.tile([P, NH], F32, tag="o", name="o")
-            nc.vector.tensor_tensor(out=o[:], in0=accs[(h, t)][:], in1=vt[h][t // 2][:, t % 2, :], op=ALU.add)
-            res[(h, t)] = o
-
-        def cast(h, t):
-            dcols = slice(h * NH, (h + 1) * NH)
-            if t % 4 == 0:
+        def K(j, h):
+            if j % 2 == 0:
                 o8s[h] = outs.tile([P, 4, NH], FP8, tag="o8", bufs=2, name="o8")
             o8 = o8s[h]
-            o = res[(h, t)]
-            nc.scalar.activation(out=o8[:, t % 4, :], in_=o[:], func=ACT.Copy, scale=Y_SCALE, saturate=False)
-            nc.sync.dma_start(out=out_0[:, t, dcols], in_=o[:])
-            if t % 4 == 3:
-                nc.sync.dma_start(out=out_1[:, t - 3:t + 1, dcols], in_=o8[:].bitcast(U8))
-            if h == 1 and t == TM - 2:
-                nc.sync.dma_start(out=out_1[:, t - 2:t + 1, dcols], in_=o8[:, 0:3, :].bitcast(U8))
+            nc.scalar.activation(out=o8[:, 2 * (j % 2):2 * (j % 2) + 2, :], in_=res[(j, h)][:], func=ACT.Copy, scale=Y_SCALE, saturate=False)
+            if j % 2 == 1:
+                nc.sync.dma_start(out=out_1[:, 2 * j - 2:2 * j + 2, h * NH:(h + 1) * NH], in_=o8[:].bitcast(U8))
 
-        def last_group():
-            h, t = 1, TM - 1
-            NQ = NH // 2
-            halves = []
-            for q in range(2):
-                acc = psum.tile([P, NQ], F32, tag="acc", bufs=3, name="accq")
-                for (l, g) in lg:
-                    bcols = slice(g * P, (g + 1) * P)
-                    dq = slice(h * NH + q * NQ, h * NH + (q + 1) * NQ)
-                    nc.tensor.matmul_mx(
-                        out=acc[:],
-                        lhsT=xq[t + l][:, bcols].bitcast(FP8X4),
-                        lhsT_scale=xsc[t + l][:, bcols],
-                        rhs=wq[l][g][:, dq].bitcast(FP8X4),
-                        rhs_scale=wsc[l][g][:, dq],
-                        start=(l == 0 and g == 0),
-                        stop=(l == 1 and g == 1),
-                    )
-                halves.append(acc)
-            for q in range(2):
-                dq = slice(h * NH + q * NQ, h * NH + (q + 1) * NQ)
-                o = outs.tile([P, NQ], F32, tag="oq", bufs=2, name="oq")
-                nc.vector.tensor_tensor(out=o[:], in0=halves[q][:], in1=vt[h][t // 2][:, t % 2, q * NQ:(q + 1) * NQ], op=ALU.add)
-                o8 = outs.tile([P, NQ], FP8, tag="o8q", bufs=2, name="o8q")
-                nc.scalar.activation(out=o8[:], in_=o[:], func=ACT.Copy, scale=Y_SCALE, saturate=False)
-                nc.sync.dma_start(out=out_0[:, t, dq], in_=o[:])
-                nc.sync.dma_start(out=out_1[:, t, dq], in_=o8[:].bitcast(U8))
 
-        lg = [(l, g) for l in range(L) for g in range(2)]
+        def last_round():
+            o = outs.tile([P, 2, NH], F32, tag="o", bufs=6, name="o")
+            o8 = o8s[1]
+            bk = {}
+            for t in (6, 7):
+                bk[t] = psum.tile([P, NH], F32, tag="acc", bufs=3, name="acc")
+                group(bk[t], 0, t, 2)
+                group(bk[t], 1, t, 3)
+            for t in (6, 7):
+                for q in range(2):
+                    nc.vector.tensor_tensor(out=o[:, t % 2, q * NQ:(q + 1) * NQ], in0=bk[t][:, q * NQ:(q + 1) * NQ], in1=vt[2 + q][3][:, t % 2, :], op=ALU.add)
+                nc.sync.dma_start(out=out_0[:, t, NH:D], in_=o[:, t % 2, :])
+                nc.scalar.activation(out=o8[:, 2 + t % 2, :], in_=o[:, t % 2, :], func=ACT.Copy, scale=Y_SCALE, saturate=False)
+                if t == 6:
+                    nc.sync.dma_start(out=out_1[:, 4:7, NH:D], in_=o8[:, 0:3, :].bitcast(U8))
+                else:
+                    nc.sync.dma_start(out=out_1[:, 7, NH:D], in_=o8[:, 3, :].bitcast(U8))
 
-        def mms(h, t):
-            acc = new_acc()
-            for (l, g) in lg:
-                mm(acc, t, h, l, g)
-            accs[(h, t)] = acc
+        def TCW(cs):
+            for c in cs:
+                for l in range(L):
+                    TW(c, l); CW(c, l)
 
-        def x_units(ts):
+        def TCX(ts):
             for t in ts:
-                unit(("x", t))
-
-        def w_units(l, g, h):
-            for cp in (2 * h, 2 * h + 1):
-                unit(("w", l, g, cp))
+                TX(t); CX(t)
 
         dummies(4)
-        x_units([0])
-        wx_spread()
-        small_transposes()
-        x_units([1, 2])
-        ctx_bias(0)
-        x_units([3, 4])
-        dummies(2)
-        w_units(0, 0, 0)
-        side_add(0, 0)
-        w_units(0, 1, 0)
-        dummies(2)
-        w_units(1, 0, 0)
-        side_add(0, 1)
-        w_units(1, 1, 0)
-        dummies(2)
-        x_units([5, 6])
-        mms(0, 0)
-        mms(0, 1)
-        add(0, 0)
-        add(0, 1)
-        x_units([7, 8])
-        side_add(0, 2)
-        cast(0, 0)
-        cast(0, 1)
-        mms(0, 2)
-        mms(0, 3)
-        add(0, 2)
-        add(0, 3)
-        side_add(0, 3)
-        w_units(0, 0, 1)
-        w_units(0, 1, 1)
-        cast(0, 2)
-        cast(0, 3)
-        mms(0, 4)
-        mms(0, 5)
-        ctx_bias(1)
-        add(0, 4)
-        add(0, 5)
-        w_units(1, 0, 1)
-        w_units(1, 1, 1)
-        side_add(1, 0)
-        cast(0, 4)
-        cast(0, 5)
-        mms(0, 6)
-        mms(0, 7)
-        add(0, 6)
-        add(0, 7)
-        side_add(1, 1)
-        cast(0, 6)
-        cast(0, 7)
-        for t in range(TM - 1):
-            mms(1, t)
-            if t in (1, 3):
-                side_add(1, (t + 3) // 2)
-            add(1, t)
-            cast(1, t)
-        last_group()
+        TCX([0, 1])
+        emb_transpose()
+        dummies(3)
+        QX(0); QX(1)
+        TCW([0, 1])
+        wxp = [wx_matmuls(0), wx_matmuls(1)]
+        wx_copy(0, wxp[0])
+        WE(0)
+        QW(0, 0); QW(0, 1)
+        TCX([2, 3])
+        wx_copy(1, wxp[1])
+        CB(0)
+        QX(2); QX(3)
+        PR(0, 0, "v")
+        M(0, 0)
+        TCX([4, 5, 6, 7, 8])
+        SA(0, 0)
+        QX(4); QX(5)
+        A(0, 0)
+        PR(1, 0, "v")
+        QX(6); QX(7); QX(8)
+        SA(1, 0)
+        wait_for(0, vt[0][1][:, 0, 0:1])
+        for j in range(4):
+            PR(j, 1)
+        for j in range(4):
+            PR(j, 2); PR(j, 3)
+        M(1, 0); M(2, 0)
+        TCW([2, 3])
+        WE(1)
+        PR(2, 0, "v")
+        A(1, 0)
+        SA(2, 0)
+        A(2, 0)
+        PR(3, 0, "v")
+        SA(3, 0)
+        QW(1, 0); QW(1, 1)
+        M(3, 0)
+        TCW([4, 5])
+        WE(2)
+        CB(1)
+        A(3, 0)
+        SA(0, 1); SA(1, 1)
+        QW(2, 0); QW(2, 1)
+        M(0, 1); M(1, 1)
+        TCW([6, 7])
+        WE(3)
+        A(0, 1); A(1, 1)
+        K(0, 0); K(1, 0)
+        SA(2, 1); SA(3, 1)
+        QW(3, 0); QW(3, 1)
+        M(2, 1); M(3, 1)
+        A(2, 1); A(3, 1)
+        CB(2); CB(3)
+        K(2, 0); K(3, 0)
+        SA(0, 3); SA(0, 2)
+        for j in range(3):
+            M(j, 2); M(j, 3)
+            A(j, 2)
+            SA(j + 1, 2)
+            A(j, 3)
+            SA(j + 1, 3)
+            K(j, 1)
+        last_round()

@@ -248,27 +248,31 @@ def tile_npchangetransitionprior_pa_kernel(tc, x, emb, Wg, bg, out_0, out_1):
         dummies(4)
         TCX([0, 1])
         emb_transpose()
-        dummies(3)
+        dummies(4)
         QX(0); QX(1)
-        TCW([0, 1])
-        wxp = [wx_matmuls(0), wx_matmuls(1)]
+        TCW([0])
+        wxp = [wx_matmuls(0)]
         wx_copy(0, wxp[0])
+        TCW([1])
+        wxp.append(wx_matmuls(1))
         WE(0)
         QW(0, 0); QW(0, 1)
-        TCX([2, 3])
+        TCX([2, 3, 4])
         wx_copy(1, wxp[1])
         CB(0)
         QX(2); QX(3)
         PR(0, 0, "v")
+        QX(4)
         M(0, 0)
-        TCX([4, 5, 6, 7, 8])
+        TCX([5, 6, 7, 8])
         SA(0, 0)
-        QX(4); QX(5)
-        A(0, 0)
         PR(1, 0, "v")
-        QX(6); QX(7); QX(8)
+        A(0, 0)
+        QX(5); QX(6)
         SA(1, 0)
-        wait_for(0, vt[0][1][:, 0, 0:1])
+        QX(7); QX(8)
+        PR(2, 0, "v")
+        wait_for(0, vt[0][2][:, 0, 0:1])
         for j in range(4):
             PR(j, 1)
         for j in range(4):
@@ -276,7 +280,6 @@ def tile_npchangetransitionprior_pa_kernel(tc, x, emb, Wg, bg, out_0, out_1):
         M(1, 0); M(2, 0)
         TCW([2, 3])
         WE(1)
-        PR(2, 0, "v")
         A(1, 0)
         SA(2, 0)
         A(2, 0)

@@ -18,7 +18,7 @@ ALU = mybir.AluOpType
 ACT = mybir.ActivationFunctionType
 
 P = 128
-LOADS = "x0 x1 e c0 c1 x2 x3 x4 x5 x6 x7 x8 x9 c2 c3 c4 c5 c6 c7"
+LOADS = "h0 h1 x0 x1 e x2 x3 x4 x5 x6 x7 x8 x9 c2 c3 c4 c5 c6 c7"
 NQ = 256
 NH = 512
 FW = H + L * D
@@ -62,6 +62,10 @@ def tile_npchangetransitionprior_pa_kernel(tc, x, emb, Wg, bg, out_0, out_1):
             elif s[0] == "x":
                 t = int(s[1])
                 nc.sync.dma_start(out=xp[t // 2][:, t % 2, :], in_=x[:, t, :])
+            elif s[0] == "h":
+                c = int(s[1])
+                nc.sync.dma_start(out=wt[c][:, 0:H + D], in_=Wg[c * P:(c + 1) * P, 0:H + D])
+                nc.sync.dma_start(out=wt[c][:, H + D:FW], in_=Wg[c * P:(c + 1) * P, H + D:FW])
             else:
                 c = int(s[1])
                 nc.sync.dma_start(out=wt[c][:], in_=Wg[c * P:(c + 1) * P, 0:FW])
@@ -246,17 +250,14 @@ def tile_npchangetransitionprior_pa_kernel(tc, x, emb, Wg, bg, out_0, out_1):
                 TX(t); CX(t)
 
         dummies(4)
-        TCX([0, 1])
-        emb_transpose()
-        dummies(4)
-        QX(0); QX(1)
-        TCW([0])
-        wxp = [wx_matmuls(0)]
-        wx_copy(0, wxp[0])
-        TCW([1])
-        wxp.append(wx_matmuls(1))
+        TCW([0, 1])
         WE(0)
+        TCX([0, 1])
         QW(0, 0); QW(0, 1)
+        QX(0); QX(1)
+        wxp = [wx_matmuls(0), wx_matmuls(1)]
+        wx_copy(0, wxp[0])
+        emb_transpose()
         TCX([2, 3, 4])
         wx_copy(1, wxp[1])
         CB(0)

@@ -98,8 +98,21 @@ def tile_npchangetransitionprior_pa_kernel(tc, x, emb, Wg, bg, out_0, out_1):
         def TX(t):
             tps[("x", t)] = four(xp[t // 2][:, t % 2, :].bitcast(F32))
 
+        wr = {}
+
+        def RW(c, l, eng):
+            wr[(c, l)] = const.tile([P, 2, 2, P], F32, name="wr%d_%d" % (c, l))
+            cp_eng(eng, wr[(c, l)][:], wt[c][:, H + l * D:H + (l + 1) * D].bitcast(F32).rearrange("p (g j u) -> p g u j", g=2, u=2))
+
         def TW(c, l):
-            tps[("w", c, l)] = four(wt[c][:, H + l * D:H + (l + 1) * D].bitcast(F32))
+            if (c, l) in wr:
+                tp = psum.tile([P, 4, P], F32, tag="tp", bufs=4, name="tp")
+                for g in range(2):
+                    for u in range(2):
+                        nc.tensor.transpose(tp[:, 2 * g + u, :], wr[(c, l)][:, g, u, :], ident_f[:])
+                tps[("w", c, l)] = tp
+            else:
+                tps[("w", c, l)] = four(wt[c][:, H + l * D:H + (l + 1) * D].bitcast(F32))
 
         def CX(t, eng="s"):
             if t % 2 == 0:
@@ -279,8 +292,10 @@ def tile_npchangetransitionprior_pa_kernel(tc, x, emb, Wg, bg, out_0, out_1):
         for j in range(4):
             PR(j, 2); PR(j, 3)
         M(1, 0); M(2, 0)
+        RW(3, 0, "s"); RW(3, 1, "s")
         TCW([2, 3])
         WE(1)
+        RW(5, 1, "s")
         A(1, 0)
         SA(2, 0)
         A(2, 0)
@@ -290,6 +305,7 @@ def tile_npchangetransitionprior_pa_kernel(tc, x, emb, Wg, bg, out_0, out_1):
         M(3, 0)
         TCW([4, 5])
         WE(2)
+        RW(7, 0, "s"); RW(7, 1, "s")
         CB(1)
         A(3, 0)
         SA(0, 1); SA(1, 1)

@@ -194,6 +194,11 @@ def tile_npchangetransitionprior_pa_kernel(tc, x, emb, Wg, bg, out_0, out_1):
         def wait_for(i, ap):
             nc.gpsimd.tensor_copy(out=junk[:, i:i + 1], in_=ap)
 
+        junk_u = const.tile([P, 8], U32, name="junk_u")
+
+        def wait_codes(i, cp):
+            nc.gpsimd.tensor_copy(out=junk_u[:, i:i + 1], in_=wq[cp][:, 3, NQ - 1:NQ])
+
         def PR(j, cp, eng="g"):
             dcols = slice(cp * NQ, (cp + 1) * NQ)
             e = nc.gpsimd if eng == "g" else nc.vector
@@ -287,10 +292,7 @@ def tile_npchangetransitionprior_pa_kernel(tc, x, emb, Wg, bg, out_0, out_1):
         QX(7); QX(8)
         PR(2, 0, "v")
         wait_for(0, vt[0][2][:, 0, 0:1])
-        for j in range(4):
-            PR(j, 1)
-        for j in range(4):
-            PR(j, 2); PR(j, 3)
+        PR(0, 1); PR(1, 1); PR(2, 1)
         M(1, 0); M(2, 0)
         RW(3, 0, "s"); RW(3, 1, "s")
         TCW([2, 3])
@@ -302,6 +304,8 @@ def tile_npchangetransitionprior_pa_kernel(tc, x, emb, Wg, bg, out_0, out_1):
         PR(3, 0, "v")
         SA(3, 0)
         QW(1, 0); QW(1, 1)
+        wait_codes(1, 1)
+        PR(3, 1); PR(0, 2); PR(0, 3)
         M(3, 0)
         TCW([4, 5])
         WE(2)
@@ -310,6 +314,8 @@ def tile_npchangetransitionprior_pa_kernel(tc, x, emb, Wg, bg, out_0, out_1):
         A(3, 0)
         SA(0, 1); SA(1, 1)
         QW(2, 0); QW(2, 1)
+        wait_codes(2, 2)
+        PR(1, 2); PR(1, 3); PR(2, 2)
         M(0, 1); M(1, 1)
         TCW([6, 7])
         WE(3)
@@ -317,6 +323,8 @@ def tile_npchangetransitionprior_pa_kernel(tc, x, emb, Wg, bg, out_0, out_1):
         K(0, 0); K(1, 0)
         SA(2, 1); SA(3, 1)
         QW(3, 0); QW(3, 1)
+        wait_codes(3, 3)
+        PR(2, 3); PR(3, 2); PR(3, 3)
         M(2, 1); M(3, 1)
         A(2, 1); A(3, 1)
         CB(2); CB(3)

@@ -77,7 +77,10 @@ def tile_npchangetransitionprior_pa_kernel(tc, x, emb, Wg, bg, out_0, out_1):
         embT = const.tile([P, B], BF16, name="embT")
         WeT = const.tile([P, D], BF16, name="WeT")
         wxB = const.tile([P, D], F32, name="wxB")
-        vt = [[const.tile([P, 2, NQ], F32, name="v%d_%d" % (cp, j)) for j in range(4)] for cp in range(4)]
+        vh = [[const.tile([P, 2, NH], F32, name="v%d_%d" % (h, j)) for j in range(4)] for h in range(2)]
+
+        def vt(j, cp):
+            return vh[cp // 2][j][:, :, (cp % 2) * NQ:(cp % 2 + 1) * NQ]
 
         def cp_eng(eng, out, in_):
             if eng == "v":
@@ -202,11 +205,11 @@ def tile_npchangetransitionprior_pa_kernel(tc, x, emb, Wg, bg, out_0, out_1):
         def PR(j, cp, eng="g"):
             dcols = slice(cp * NQ, (cp + 1) * NQ)
             e = nc.gpsimd if eng == "g" else nc.vector
-            e.tensor_tensor(out=vt[cp][j][:], in0=xp[j + 1][:, :, dcols], in1=wxB[:, dcols].unsqueeze(1).to_broadcast([P, 2, NQ]), op=ALU.mult)
+            e.tensor_tensor(out=vt(j, cp), in0=xp[j + 1][:, :, dcols], in1=wxB[:, dcols].unsqueeze(1).to_broadcast([P, 2, NQ]), op=ALU.mult)
 
         def SA(j, cp):
             cps = cbank[min(cp, 2)][:, (cp // 3) * NQ:(cp // 3 + 1) * NQ]
-            nc.vector.tensor_tensor(out=vt[cp][j][:], in0=vt[cp][j][:], in1=cps.unsqueeze(1).to_broadcast([P, 2, NQ]), op=ALU.add)
+            nc.vector.tensor_tensor(out=vt(j, cp), in0=vt(j, cp), in1=cps.unsqueeze(1).to_broadcast([P, 2, NQ]), op=ALU.add)
 
         banks = {}
         res = {}
@@ -225,7 +228,7 @@ def tile_npchangetransitionprior_pa_kernel(tc, x, emb, Wg, bg, out_0, out_1):
             nc.vector.tensor_tensor(
                 out=res[(j, h)][:, :, q * NQ:(q + 1) * NQ],
                 in0=banks[(j, cp)][:].rearrange("p (s n) -> p s n", s=2),
-                in1=vt[cp][j][:],
+                in1=vt(j, cp),
                 op=ALU.add,
             )
             if q == 1:
@@ -240,23 +243,40 @@ def tile_npchangetransitionprior_pa_kernel(tc, x, emb, Wg, bg, out_0, out_1):
                 nc.sync.dma_start(out=out_1[:, 2 * j - 2:2 * j + 2, h * NH:(h + 1) * NH], in_=o8[:].bitcast(U8))
 
 
-        def last_round():
-            o = outs.tile([P, 2, NH], F32, tag="o", bufs=6, name="o")
-            o8 = o8s[1]
-            bk = {}
-            for t in (6, 7):
-                bk[t] = psum.tile([P, NH], F32, tag="acc", bufs=3, name="acc")
-                group(bk[t], 0, t, 2)
-                group(bk[t], 1, t, 3)
-            for t in (6, 7):
+        def MT(t, cp):
+            if t not in banks:
+                banks[t] = psum.tile([P, NH], F32, tag="acc", bufs=3, name="acc")
+            group(banks[t], cp - 2, t, cp)
+
+        def AT(t):
+            j, s = t // 2, t % 2
+            if s == 0:
+                res[(j, 1)] = outs.tile([P, 2, NH], F32, tag="o", bufs=6, name="o")
+            o = res[(j, 1)]
+            if t < 7:
+                nc.vector.tensor_tensor(out=o[:, s, :], in0=banks[t][:], in1=vh[1][j][:, s, :], op=ALU.add)
+            else:
                 for q in range(2):
-                    nc.vector.tensor_tensor(out=o[:, t % 2, q * NQ:(q + 1) * NQ], in0=bk[t][:, q * NQ:(q + 1) * NQ], in1=vt[2 + q][3][:, t % 2, :], op=ALU.add)
-                nc.sync.dma_start(out=out_0[:, t, NH:D], in_=o[:, t % 2, :])
-                nc.scalar.activation(out=o8[:, 2 + t % 2, :], in_=o[:, t % 2, :], func=ACT.Copy, scale=Y_SCALE, saturate=False)
-                if t == 6:
-                    nc.sync.dma_start(out=out_1[:, 4:7, NH:D], in_=o8[:, 0:3, :].bitcast(U8))
-                else:
-                    nc.sync.dma_start(out=out_1[:, 7, NH:D], in_=o8[:, 3, :].bitcast(U8))
+                    cols = slice(q * NQ, (q + 1) * NQ)
+                    nc.vector.tensor_tensor(out=o[:, s, cols], in0=banks[t][:, cols], in1=vh[1][j][:, s, cols], op=ALU.add)
+            nc.sync.dma_start(out=out_0[:, t, NH:D], in_=o[:, s, :])
+
+        def KT(t):
+            j, s = t // 2, t % 2
+            if t % 4 == 0:
+                o8s[1] = outs.tile([P, 4, NH], FP8, tag="o8", bufs=2, name="o8")
+            o, o8 = res[(j, 1)], o8s[1]
+            if t < 7:
+                nc.scalar.activation(out=o8[:, t % 4, :], in_=o[:, s, :], func=ACT.Copy, scale=Y_SCALE, saturate=False)
+            else:
+                nc.scalar.activation(out=o8[:, 3, 0:NQ], in_=o[:, 1, 0:NQ], func=ACT.Copy, scale=Y_SCALE, saturate=False)
+                nc.vector.tensor_scalar(out=o8[:, 3, NQ:NH], in0=o[:, 1, NQ:NH], scalar1=Y_SCALE, scalar2=None, op0=ALU.mult, saturate=False)
+            if t == 3:
+                nc.sync.dma_start(out=out_1[:, 0:4, NH:D], in_=o8[:].bitcast(U8))
+            elif t == 6:
+                nc.sync.dma_start(out=out_1[:, 4:7, NH:D], in_=o8[:, 0:3, :].bitcast(U8))
+            elif t == 7:
+                nc.sync.dma_start(out=out_1[:, 7, NH:D], in_=o8[:, 3, :].bitcast(U8))
 
         def TCW(cs):
             for c in cs:
@@ -291,7 +311,7 @@ def tile_npchangetransitionprior_pa_kernel(tc, x, emb, Wg, bg, out_0, out_1):
         SA(1, 0)
         QX(7); QX(8)
         PR(2, 0, "v")
-        wait_for(0, vt[0][2][:, 0, 0:1])
+        wait_for(0, vt(2, 0)[:, 0, 0:1])
         PR(0, 1); PR(1, 1); PR(2, 1)
         M(1, 0); M(2, 0)
         RW(3, 0, "s"); RW(3, 1, "s")
@@ -329,12 +349,26 @@ def tile_npchangetransitionprior_pa_kernel(tc, x, emb, Wg, bg, out_0, out_1):
         A(2, 1); A(3, 1)
         CB(2); CB(3)
         K(2, 0); K(3, 0)
-        SA(0, 3); SA(0, 2)
-        for j in range(3):
-            M(j, 2); M(j, 3)
-            A(j, 2)
-            SA(j + 1, 2)
-            A(j, 3)
-            SA(j + 1, 3)
-            K(j, 1)
-        last_round()
+        SA(0, 2); SA(0, 3)
+        MT(0, 2); MT(1, 2)
+        MT(0, 3); MT(1, 3)
+        SA(1, 2)
+        AT(0); KT(0)
+        SA(1, 3)
+        AT(1); KT(1)
+        SA(2, 2)
+        MT(2, 2); MT(2, 3)
+        AT(2); KT(2)
+        SA(2, 3)
+        MT(3, 2); MT(3, 3)
+        AT(3); KT(3)
+        SA(3, 2)
+        MT(4, 2); MT(4, 3)
+        AT(4); KT(4)
+        SA(3, 3)
+        MT(5, 2); MT(5, 3)
+        AT(5); KT(5)
+        MT(6, 2); MT(6, 3)
+        AT(6); KT(6)
+        MT(7, 2); MT(7, 3)
+        AT(7); KT(7)

from contextlib import ExitStack

import concourse.mybir as mybir
from concourse.masks import make_identity

B, T, D, H, L = 128, 10, 1024, 128, 2
TM = T - L
Y_SCALE = 210.0
FLOPS = 2 * B * TM * D * (L * D) + 2 * B * H * D

F32 = mybir.dt.float32
BF16 = mybir.dt.bfloat16
U32 = mybir.dt.uint32
U8 = mybir.dt.uint8
FP8X4 = mybir.dt.float8_e4m3fn_x4
FP8 = mybir.dt.float8_e4m3fn
ALU = mybir.AluOpType
ACT = mybir.ActivationFunctionType

P = 128
LOADS = "h0 h1 x0 x1 e x2 x3 x4 x5 x6 x7 x8 x9 c2 c3 c4 c5 c6 c7"
NQ = 256
NH = 512
FW = H + L * D


def tile_npchangetransitionprior_pa_kernel(tc, x, emb, Wg, bg, out_0, out_1):
    nc = tc.nc
    with ExitStack() as ctx:
        const = ctx.enter_context(tc.tile_pool(name="const", bufs=1))
        stage = ctx.enter_context(tc.tile_pool(name="stage", bufs=2))
        outs = ctx.enter_context(tc.tile_pool(name="outs", bufs=6))
        psum = ctx.enter_context(tc.psum_pool(name="psum", bufs=1))
        ctx.enter_context(tc.manual_schedule())

        warm = const.tile([P, NH], BF16, name="warm")
        nc.vector.memset(warm[:], 0.0)
        ones = const.tile([P, P], BF16, name="ones")
        nc.vector.memset(ones[:], 1.0)
        tiny = const.tile([P, 2], F32, name="tiny")
        nc.vector.memset(tiny[:], 0.0)
        ident_f = const.tile([P, P], F32, name="ident_f")
        make_identity(nc, ident_f[:])
        ident_b = const.tile([P, P], BF16, name="ident_b")
        make_identity(nc, ident_b[:])
        bgz = const.tile([P, D], BF16, name="bgz")
        nc.vector.memset(bgz[:], 0.0)

        xp = [const.tile([P, 2, D], BF16, name="xp%d" % j) for j in range(T // 2)]
        wt = [const.tile([P, FW], BF16, name="wt%d" % c) for c in range(8)]
        emb_sb = const.tile([P, H], BF16, name="emb_sb")
        wx_sb = const.tile([P, 8], BF16, name="wx_sb")

        nc.scalar.activation(out=tiny[:, 1:2], in_=tiny[:, 0:1], func=ACT.Copy)

        for s in LOADS.split():
            if s == "e":
                with nc.allow_non_contiguous_dma(reason="one weight of each row of Wg"):
                    nc.sync.dma_start(out=wx_sb[:], in_=Wg[:, FW:FW + 1].rearrange("(c p) o -> p (c o)", p=P))
                nc.sync.dma_start(out=emb_sb[:], in_=emb[:, :])
                nc.sync.dma_start(out=bgz[0:1, :], in_=bg.unsqueeze(0))
            elif s[0] == "x":
                t = int(s[1])
                nc.sync.dma_start(out=xp[t // 2][:, t % 2, :], in_=x[:, t, :])
            elif s[0] == "h":
                c = int(s[1])
                nc.sync.dma_start(out=wt[c][:, 0:H + D], in_=Wg[c * P:(c + 1) * P, 0:H + D])
                nc.sync.dma_start(out=wt[c][:, H + D:FW], in_=Wg[c * P:(c + 1) * P, H + D:FW])
            else:
                c = int(s[1])
                nc.sync.dma_start(out=wt[c][:], in_=Wg[c * P:(c + 1) * P, 0:FW])

        xq = [const.tile([P, 2, 256], U32, name="xq%d" % j, align_bytes=64) for j in range(T // 2)]
        xsc = [const.tile([P, 2, 256], U8, name="xsc%d" % j, align_bytes=64) for j in range(T // 2)]
        wq = [const.tile([P, 4, NQ], U32, name="wq%d" % cp, align_bytes=64) for cp in range(4)]
        wsc = [const.tile([P, 4, NQ], U8, name="wsc%d" % cp, align_bytes=64) for cp in range(4)]
        embT = const.tile([P, B], BF16, name="embT")
        WeT = const.tile([P, D], BF16, name="WeT")
        wxB = const.tile([P, D], F32, name="wxB")
        vh = [[const.tile([P, 2, NH], F32, name="v%d_%d" % (h, j)) for j in range(4)] for h in range(2)]

        def vt(j, cp):
            return vh[cp // 2][j][:, :, (cp % 2) * NQ:(cp % 2 + 1) * NQ]

        def cp_eng(eng, out, in_):
            if eng == "v":
                nc.vector.tensor_copy(out=out, in_=in_)
            else:
                nc.scalar.copy(out=out, in_=in_)

        tps = {}
        grps = {}

        def four(words):
            tp = psum.tile([P, 4, P], F32, tag="tp", bufs=4, name="tp")
            for g in range(2):
                for u in range(2):
                    nc.tensor.transpose(tp[:, 2 * g + u, :], words[:, 256 * g + u:256 * (g + 1):2], ident_f[:])
            return tp

        def TX(t):
            tps[("x", t)] = four(xp[t // 2][:, t % 2, :].bitcast(F32))

        wr = {}

        def RW(c, l, eng):
            wr[(c, l)] = const.tile([P, 2, 2, P], F32, name="wr%d_%d" % (c, l))
            cp_eng(eng, wr[(c, l)][:], wt[c][:, H + l * D:H + (l + 1) * D].bitcast(F32).rearrange("p (g j u) -> p g u j", g=2, u=2))

        def TW(c, l):
            if (c, l) in wr:
                tp = psum.tile([P, 4, P], F32, tag="tp", bufs=4, name="tp")
                for g in range(2):
                    for u in range(2):
                        nc.tensor.transpose(tp[:, 2 * g + u, :], wr[(c, l)][:, g, u, :], ident_f[:])
                tps[("w", c, l)] = tp
            else:
                tps[("w", c, l)] = four(wt[c][:, H + l * D:H + (l + 1) * D].bitcast(F32))

        def CX(t, eng="s"):
            if t % 2 == 0:
                grps[("x", t // 2)] = stage.tile([P, 2, 1024], BF16, tag="grpx", bufs=3, name="grpx", align_bytes=64)
            dst = grps[("x", t // 2)][:, t % 2, :].bitcast(F32).rearrange("p (g r u) -> p g r u", g=2, u=2)
            cp_eng(eng, dst, tps[("x", t)][:].rearrange("p (g u) r -> p g r u", u=2))

        def CW(c, l, eng="s"):
            cp, ci = c // 2, c % 2
            if ci == 0:
                grps[(cp, l)] = stage.tile([P, 2, 2, 512], BF16, tag="grpw", bufs=4, name="grpw", align_bytes=64)
            dst = grps[(cp, l)][:, :, ci, :].bitcast(F32).rearrange("p g (r u) -> p g r u", u=2)
            cp_eng(eng, dst, tps[("w", c, l)][:].rearrange("p (g u) r -> p g r u", u=2))

        def QX(t):
            nc.vector.quantize_mx(out=xq[t // 2][:, t % 2, :].bitcast(FP8X4), scales=xsc[t // 2][:, t % 2, :], in_=grps[("x", t // 2)][:, t % 2, :])

        def QW(cp, l):
            nc.vector.quantize_mx(
                out=wq[cp][:, 2 * l:2 * l + 2, :].rearrange("p a r -> p (a r)").bitcast(FP8X4),
                scales=wsc[cp][:, 2 * l:2 * l + 2, :].rearrange("p a r -> p (a r)"),
                in_=grps[(cp, l)][:].rearrange("p g c r -> p (g c r)"),
            )

        def group(bank, slot, t, cp):
            for a in range(4):
                l, g = a // 2, a % 2
                s = t + l
                bcols = slice(g * P, (g + 1) * P)
                nc.tensor.matmul_mx(
                    out=bank[:, slot * NQ:(slot + 1) * NQ],
                    lhsT=xq[s // 2][:, s % 2, bcols].bitcast(FP8X4),
                    lhsT_scale=xsc[s // 2][:, s % 2, bcols],
                    rhs=wq[cp][:, a, :].bitcast(FP8X4),
                    rhs_scale=wsc[cp][:, a, :],
                    start=(a == 0),
                    stop=(a == 3),
                )

        def dummies(n):
            wps = psum.tile([P, NH], F32, tag="acc", bufs=3, name="wps")
            for i in range(n):
                nc.tensor.matmul(wps[:], lhsT=ones[:], rhs=warm[:], start=True, stop=True)

        def emb_transpose():
            tpe = psum.tile([P, B], BF16, tag="tp", bufs=4, name="tpe")
            nc.tensor.transpose(tpe[:], emb_sb[:], ident_b[:])
            nc.scalar.copy(out=embT[:], in_=tpe[:])

        def wx_matmuls(h):
            wxp = psum.tile([P, NH], F32, tag="acc", bufs=3, name="wxp")
            for ci in range(4):
                c = 4 * h + ci
                nc.tensor.matmul(wxp[:, ci * P:(ci + 1) * P], lhsT=wx_sb[:, c:c + 1].to_broadcast([P, P]), rhs=ident_b[:], start=True, stop=True)
            return wxp

        def wx_copy(h, wxp):
            nc.scalar.copy(out=wxB[:, h * NH:(h + 1) * NH], in_=wxp[:])

        cbank = {}

        def WE(cp):
            dcols = slice(cp * NQ, (cp + 1) * NQ)
            tpw = psum.tile([P, NQ], BF16, tag="tp", bufs=4, name="tpw")
            for ci in range(2):
                nc.tensor.transpose(tpw[:, ci * P:(ci + 1) * P], wt[2 * cp + ci][:, 0:H], ident_b[:])
            nc.scalar.copy(out=WeT[:, dcols], in_=tpw[:])

        def CB(cp):
            dcols = slice(cp * NQ, (cp + 1) * NQ)
            if cp < 3:
                cbank[min(cp, 2)] = psum.tile([P, NH], F32, tag="cb", bufs=1, name="cps")
            cps = cbank[min(cp, 2)][:, (cp // 3) * NQ:(cp // 3 + 1) * NQ]
            nc.tensor.matmul(cps, lhsT=embT[:], rhs=WeT[:, dcols], start=True, stop=False)
            nc.tensor.matmul(cps, lhsT=ones[:], rhs=bgz[:, dcols], start=False, stop=True)

        junk = const.tile([P, 8], F32, name="junk")

        def wait_for(i, ap):
            nc.gpsimd.tensor_copy(out=junk[:, i:i + 1], in_=ap)

        junk_u = const.tile([P, 8], U32, name="junk_u")

        def wait_codes(i, cp):
            nc.gpsimd.tensor_copy(out=junk_u[:, i:i + 1], in_=wq[cp][:, 3, NQ - 1:NQ])

        def PR(j, cp, eng="g"):
            dcols = slice(cp * NQ, (cp + 1) * NQ)
            e = nc.gpsimd if eng == "g" else nc.vector
            e.tensor_tensor(out=vt(j, cp), in0=xp[j + 1][:, :, dcols], in1=wxB[:, dcols].unsqueeze(1).to_broadcast([P, 2, NQ]), op=ALU.mult)

        def SA(j, cp):
            cps = cbank[min(cp, 2)][:, (cp // 3) * NQ:(cp // 3 + 1) * NQ]
            nc.vector.tensor_tensor(out=vt(j, cp), in0=vt(j, cp), in1=cps.unsqueeze(1).to_broadcast([P, 2, NQ]), op=ALU.add)

        banks = {}
        res = {}
        o8s = {}

        def M(j, cp):
            bank = psum.tile([P, NH], F32, tag="acc", bufs=3, name="acc")
            group(bank, 0, 2 * j, cp)
            group(bank, 1, 2 * j + 1, cp)
            banks[(j, cp)] = bank

        def A(j, cp):
            h, q = cp // 2, cp % 2
            if q == 0:
                res[(j, h)] = outs.tile([P, 2, NH], F32, tag="o", bufs=6, name="o")
            nc.vector.tensor_tensor(
                out=res[(j, h)][:, :, q * NQ:(q + 1) * NQ],
                in0=banks[(j, cp)][:].rearrange("p (s n) -> p s n", s=2),
                in1=vt(j, cp),
                op=ALU.add,
            )
            if q == 1:
                nc.sync.dma_start(out=out_0[:, 2 * j:2 * j + 2, h * NH:(h + 1) * NH], in_=res[(j, h)][:])

        def K(j, h):
            if j % 2 == 0:
                o8s[h] = outs.tile([P, 4, NH], FP8, tag="o8", bufs=2, name="o8")
            o8 = o8s[h]
            nc.scalar.activation(out=o8[:, 2 * (j % 2):2 * (j % 2) + 2, :], in_=res[(j, h)][:], func=ACT.Copy, scale=Y_SCALE, saturate=False)
            if j % 2 == 1:
                nc.sync.dma_start(out=out_1[:, 2 * j - 2:2 * j + 2, h * NH:(h + 1) * NH], in_=o8[:].bitcast(U8))


        def MT(t, cp):
            if t not in banks:
                banks[t] = psum.tile([P, NH], F32, tag="acc", bufs=3, name="acc")
            group(banks[t], cp - 2, t, cp)

        def AT(t):
            j, s = t // 2, t % 2
            if s == 0:
                res[(j, 1)] = outs.tile([P, 2, NH], F32, tag="o", bufs=6, name="o")
            o = res[(j, 1)]
            if t < 7:
                nc.vector.tensor_tensor(out=o[:, s, :], in0=banks[t][:], in1=vh[1][j][:, s, :], op=ALU.add)
            else:
                for q in range(2):
                    cols = slice(q * NQ, (q + 1) * NQ)
                    nc.vector.tensor_tensor(out=o[:, s, cols], in0=banks[t][:, cols], in1=vh[1][j][:, s, cols], op=ALU.add)
            nc.sync.dma_start(out=out_0[:, t, NH:D], in_=o[:, s, :])

        def KT(t):
            j, s = t // 2, t % 2
            if t % 4 == 0:
                o8s[1] = outs.tile([P, 4, NH], FP8, tag="o8", bufs=2, name="o8")
            o, o8 = res[(j, 1)], o8s[1]
            if t < 7:
                nc.scalar.activation(out=o8[:, t % 4, :], in_=o[:, s, :], func=ACT.Copy, scale=Y_SCALE, saturate=False)
            else:
                nc.scalar.activation(out=o8[:, 3, 0:NQ], in_=o[:, 1, 0:NQ], func=ACT.Copy, scale=Y_SCALE, saturate=False)
                nc.vector.tensor_scalar(out=o8[:, 3, NQ:NH], in0=o[:, 1, NQ:NH], scalar1=Y_SCALE, scalar2=None, op0=ALU.mult, saturate=False)
            if t == 3:
                nc.sync.dma_start(out=out_1[:, 0:4, NH:D], in_=o8[:].bitcast(U8))
            elif t == 6:
                nc.sync.dma_start(out=out_1[:, 4:7, NH:D], in_=o8[:, 0:3, :].bitcast(U8))
            elif t == 7:
                nc.sync.dma_start(out=out_1[:, 7, NH:D], in_=o8[:, 3, :].bitcast(U8))

        def TCW(cs):
            for c in cs:
                for l in range(L):
                    TW(c, l); CW(c, l)

        def TCX(ts):
            for t in ts:
                TX(t); CX(t)

        dummies(4)
        TCW([0, 1])
        WE(0)
        TCX([0, 1])
        QW(0, 0); QW(0, 1)
        QX(0); QX(1)
        wxp = [wx_matmuls(0), wx_matmuls(1)]
        wx_copy(0, wxp[0])
        emb_transpose()
        TCX([2, 3, 4])
        wx_copy(1, wxp[1])
        CB(0)
        QX(2); QX(3)
        PR(0, 0, "v")
        QX(4)
        M(0, 0)
        TCX([5, 6, 7, 8])
        SA(0, 0)
        PR(1, 0, "v")
        A(0, 0)
        QX(5); QX(6)
        SA(1, 0)
        QX(7); QX(8)
        PR(2, 0, "v")
        wait_for(0, vt(2, 0)[:, 0, 0:1])
        PR(0, 1); PR(1, 1); PR(2, 1)
        M(1, 0); M(2, 0)
        RW(3, 0, "s"); RW(3, 1, "s")
        TCW([2, 3])
        WE(1)
        RW(5, 1, "s")
        A(1, 0)
        SA(2, 0)
        A(2, 0)
        PR(3, 0, "v")
        SA(3, 0)
        QW(1, 0); QW(1, 1)
        wait_codes(1, 1)
        PR(3, 1); PR(0, 2); PR(0, 3)
        M(3, 0)
        TCW([4, 5])
        WE(2)
        RW(7, 0, "s"); RW(7, 1, "s")
        CB(1)
        A(3, 0)
        SA(0, 1); SA(1, 1)
        QW(2, 0); QW(2, 1)
        wait_codes(2, 2)
        PR(1, 2); PR(1, 3); PR(2, 2)
        M(0, 1); M(1, 1)
        TCW([6, 7])
        WE(3)
        A(0, 1); A(1, 1)
        K(0, 0); K(1, 0)
        SA(2, 1); SA(3, 1)
        QW(3, 0); QW(3, 1)
        wait_codes(3, 3)
        PR(2, 3); PR(3, 2); PR(3, 3)
        M(2, 1); M(3, 1)
        A(2, 1); A(3, 1)
        CB(2); CB(3)
        K(2, 0); K(3, 0)
        SA(0, 2); SA(0, 3)
        MT(0, 2); MT(1, 2)
        MT(0, 3); MT(1, 3)
        SA(1, 2)
        AT(0); KT(0)
        SA(1, 3)
        AT(1); KT(1)
        SA(2, 2)
        MT(2, 2); MT(2, 3)
        AT(2); KT(2)
        SA(2, 3)
        MT(3, 2); MT(3, 3)
        AT(3); KT(3)
        SA(3, 2)
        MT(4, 2); MT(4, 3)
        AT(4); KT(4)
        SA(3, 3)
        MT(5, 2); MT(5, 3)
        AT(5); KT(5)
        MT(6, 2); MT(6, 3)
        AT(6); KT(6)
        MT(7, 2); MT(7, 3)
        AT(7); KT(7)
